import numpy as np
import ml_dtypes


def mxq(x, axis, fmt="e4m3"):
    dtype, down = {"e4m3": (ml_dtypes.float8_e4m3fn, 7), "e5m2": (ml_dtypes.float8_e5m2, 14)}[fmt]
    v = np.moveaxis(np.asarray(x, np.float32).astype(ml_dtypes.bfloat16).astype(np.float64), axis, -1)
    blocks = v.reshape(v.shape[:-1] + (-1, 32))
    amax = np.abs(blocks).max(-1, keepdims=True)
    byte = np.maximum(np.where(amax > 0, np.frexp(amax)[1] - 1 + 127, 0) - down, 1)
    scale = np.exp2(byte - 127.0)
    codes = (blocks / scale).astype(np.float32).astype(dtype).astype(np.float64)
    return np.moveaxis((codes * scale).reshape(v.shape), -1, axis)


WIDE = False


def mx_kscale(k):
    if not WIDE:
        return np.ones(k)
    levels = np.array([20, -20, 10, -10, 0])
    a = np.random.permutation(np.resize(levels, k // 512 * 4)).reshape(k // 512, 4)
    idx = np.arange(k)
    return np.exp2(a[idx // 512, idx % 128 // 32])


BF16 = ml_dtypes.bfloat16


def bf(x):
    return np.asarray(x, np.float32).astype(BF16)


def f64(x):
    return np.asarray(x).astype(np.float64)


N, N_CH, D, H = 512, 4, 4, 512


def sigmoid(v):
    return 1.0 / (1.0 + np.exp(-v))


def setup_inputs():
    s = mx_kscale(H)
    neighbour_h = bf(np.random.standard_normal((N, N_CH, H)))
    neighbour_c = bf(np.random.standard_normal((N, N_CH, H)))
    f_input = bf(np.random.standard_normal((N, H)))
    iou_input = bf(np.random.standard_normal((N, 3 * H)) * 0.5)
    U_f0 = bf(np.random.standard_normal((D, H, H)) * 0.8 / np.sqrt(H))
    U_iou0 = bf(np.random.standard_normal((D, 3 * H, H)) * 1.6 / np.sqrt(D * H))
    g = bf(np.random.standard_normal((2, N, H)) * np.exp2(np.random.randint(-12, 1, (1, N, 1))) * 32.0 * s)
    nh = f64(neighbour_h)
    f_logits = (nh.transpose(1, 0, 2) @ f64(U_f0).transpose(0, 2, 1)).transpose(1, 0, 2) + f64(f_input)[:, None, :]
    iou = nh.reshape(N, D * H) @ f64(U_iou0).transpose(0, 2, 1).reshape(D * H, 3 * H) + 2.0 * f64(iou_input)
    i, o, u = np.split(iou, 3, axis=1)
    c = sigmoid(i) * np.tanh(u) + np.sum(sigmoid(f_logits) * f64(neighbour_c), axis=1)
    return {
        "neighbour_h": neighbour_h,
        "neighbour_c": neighbour_c,
        "f_input": f_input,
        "iou_input": iou_input,
        "U_f": bf(f64(U_f0) / s[None, :, None]),
        "U_iou": bf(f64(U_iou0) / np.tile(s, 3)[None, :, None]),
        "f_logits": np.asarray(f_logits, np.float32),
        "iou": np.asarray(iou, np.float32),
        "c": np.asarray(c, np.float32),
        "grad_out": g,
    }


def reference(neighbour_h, neighbour_c, f_input, iou_input, U_f, U_iou, f_logits, iou, c, grad_out):
    g = f64(grad_out)
    gh, gc = g[0], g[1]
    i, o, u = np.split(f64(iou), 3, axis=1)
    si, so, tu, tc = sigmoid(i), sigmoid(o), np.tanh(u), np.tanh(f64(c))
    dc = gc + gh * so * (1.0 - tc * tc)
    di = dc * tu * si * (1.0 - si)
    do = gh * tc * so * (1.0 - so)
    du = dc * si * (1.0 - tu * tu)
    diou = np.concatenate([di, do, du], axis=1)
    f = sigmoid(f64(f_logits))
    df = dc[:, None, :] * f64(neighbour_c) * f * (1.0 - f)
    part_f = mxq(df.transpose(1, 0, 2), 2, "e5m2") @ mxq(f64(U_f), 1, "e4m3")
    w_iou = f64(U_iou).transpose(1, 0, 2).reshape(3 * H, D * H)
    part_iou = mxq(diou, 1, "e5m2") @ mxq(w_iou, 0, "e4m3")
    return part_f.transpose(1, 0, 2) + part_iou.reshape(N, D, H)

@@ -1,0 +1,235 @@
+from contextlib import ExitStack
+
+import concourse.mybir as mybir
+from concourse.masks import make_identity
+
+F32 = mybir.dt.float32
+BF16 = mybir.dt.bfloat16
+U32 = mybir.dt.uint32
+U8 = mybir.dt.uint8
+E4M3X4 = mybir.dt.float8_e4m3fn_x4
+E5M2X4 = mybir.dt.float8_e5m2_x4
+ACT = mybir.ActivationFunctionType
+ALU = mybir.AluOpType
+
+P = 128
+PACK = 4
+K_PASS = P * PACK
+NODES = 512
+CHILDREN = 4
+HID = 512
+NODE_TILES = NODES // P
+GATES = 3
+W_CHUNKS = 1 + GATES
+A_PASSES = GATES + CHILDREN
+
+VECTOR_COLS = 192
+
+FLOPS = 2 * NODES * CHILDREN * HID * (HID + GATES * HID)
+BYTES = (
+    2 * NODES * CHILDREN * HID
+    + 2 * CHILDREN * (1 + GATES) * HID * HID
+    + 4 * NODES * (CHILDREN + GATES + 1) * HID
+    + 2 * 2 * NODES * HID
+    + 4 * NODES * CHILDREN * HID
+)
+
+
+def tile_generictreelstmcell_t_v_kernel(
+    tc, neighbour_h, neighbour_c, f_input, iou_input, U_f, U_iou, f_logits, iou, c, grad_out, out
+):
+    nc = tc.nc
+
+    fl_v = f_logits.rearrange("(a p) d k -> a p (d k)", p=P)
+    nc_v = neighbour_c.rearrange("(a p) d k -> a p (d k)", p=P)
+    iou_v = iou.rearrange("(a p) j -> a p j", p=P)
+    c_v = c.rearrange("(a p) k -> a p k", p=P)
+    g_v = grad_out.rearrange("g (a p) k -> a p g k", p=P)
+    out_v = out.rearrange("(a p) d h -> a p d h", p=P)
+    uf_v = U_f.rearrange("d (t p) h -> d p t h", p=P)
+    ui_v = U_iou.rearrange("d (g t p) h -> d g p t h", p=P, t=PACK)
+
+    with ExitStack() as ctx:
+        consts = ctx.enter_context(tc.tile_pool(name="consts", bufs=1))
+        keep = ctx.enter_context(tc.tile_pool(name="keep", bufs=1))
+        raw_a = ctx.enter_context(tc.tile_pool(name="raw_a", bufs=2))
+        raw_w = ctx.enter_context(tc.tile_pool(name="raw_w", bufs=8))
+        grp = ctx.enter_context(tc.tile_pool(name="grp", bufs=3))
+        xs = ctx.enter_context(tc.tile_pool(name="xs", bufs=2))
+        xv = ctx.enter_context(tc.tile_pool(name="xv", bufs=1))
+        fs = ctx.enter_context(tc.tile_pool(name="fs", bufs=3))
+        bfp = ctx.enter_context(tc.tile_pool(name="bfp", bufs=2))
+        outp = ctx.enter_context(tc.tile_pool(name="outp", bufs=4))
+        tp32 = ctx.enter_context(tc.psum_pool(name="tp32", bufs=3))
+        tp16 = ctx.enter_context(tc.psum_pool(name="tp16", bufs=2))
+        accp = ctx.enter_context(tc.psum_pool(name="accp", bufs=3))
+
+        ident32 = consts.tile([P, P], F32)
+        make_identity(nc, ident32[:])
+        ident16 = consts.tile([P, P], BF16)
+        make_identity(nc, ident16[:])
+
+        w_codes = keep.tile([P, CHILDREN, W_CHUNKS, HID], U32, align_bytes=64)
+        w_scales = keep.tile([P, CHILDREN, W_CHUNKS, HID], U8, align_bytes=64)
+        a_codes = keep.tile([P, NODE_TILES, A_PASSES, P], U32, align_bytes=64)
+        a_scales = keep.tile([P, NODE_TILES, A_PASSES, P], U8, align_bytes=64)
+
+        def load_weights(d):
+            chunks = []
+            for q in range(W_CHUNKS):
+                w_raw = raw_w.tile([P, PACK, HID], BF16, name="w_raw")
+                nc.sync.dma_start(out=w_raw[:], in_=uf_v[d] if q == 0 else ui_v[d, q - 1])
+                chunks.append(w_raw)
+            return chunks
+
+        def quantise_weights(d, chunks):
+            for q in range(W_CHUNKS):
+                grouped = grp.tile([P, HID, PACK], BF16, name="grouped", align_bytes=64)
+                for engine_copy, h0, h1 in (
+                    (nc.vector.tensor_copy, 0, VECTOR_COLS),
+                    (nc.scalar.copy, VECTOR_COLS, HID),
+                ):
+                    engine_copy(
+                        out=grouped[:, h0:h1, :].rearrange("p (c i) t -> p c t i", i=4),
+                        in_=chunks[q][:, :, h0:h1].rearrange("p t (c i) -> p c t i", i=4),
+                    )
+                nc.vector.quantize_mx(
+                    out=w_codes[:, d, q, :].bitcast(E4M3X4),
+                    scales=w_scales[:, d, q, :],
+                    in_=grouped[:].rearrange("p h t -> p (h t)"),
+                )
+
+        def load_gate_inputs(a):
+            iou_sb = raw_a.tile([P, GATES * HID], F32, name="iou_sb")
+            nc.sync.dma_start(out=iou_sb[:], in_=iou_v[a])
+            c_sb = raw_a.tile([P, HID], F32, name="c_sb")
+            nc.sync.dma_start(out=c_sb[:], in_=c_v[a])
+            g_sb = raw_a.tile([P, 2, HID], BF16, name="g_sb")
+            nc.sync.dma_start(out=g_sb[:], in_=g_v[a])
+            return iou_sb, c_sb, g_sb
+
+        def load_forget_inputs(a):
+            fl_sb = raw_a.tile([P, CHILDREN * HID], F32, name="fl_sb")
+            nc.sync.dma_start(out=fl_sb[:], in_=fl_v[a])
+            nc_sb = raw_a.tile([P, CHILDREN * HID], BF16, name="nc_sb")
+            nc.sync.dma_start(out=nc_sb[:], in_=nc_v[a])
+            return fl_sb, nc_sb
+
+        def transpose_512(bank, src, ident):
+            for t in range(PACK):
+                nc.tensor.transpose(bank[:, t, :], src[:, t * P : (t + 1) * P], ident[:])
+
+        def by_node(bank):
+            return bank.rearrange("p t n -> p n t")
+
+        def tanh_of(src, scale, pool, name):
+            bank = tp32.tile([P, PACK, P], F32, name="bank32")
+            transpose_512(bank, src, ident32)
+            res = pool.tile([P, P, PACK], F32, name=name)
+            nc.scalar.activation(out=res[:], in_=by_node(bank[:]), func=ACT.Tanh, scale=scale)
+            return res
+
+        def square_of(src, scale, pool, name):
+            res = pool.tile([P, P, PACK], F32, name=name)
+            nc.scalar.activation(out=res[:], in_=src[:], func=ACT.Square, scale=scale)
+            return res
+
+        def fused(out_ap, in0, scalar, op0, in1, op1):
+            nc.vector.scalar_tensor_tensor(out=out_ap, in0=in0, scalar=scalar, in1=in1, op0=op0, op1=op1)
+
+        def quantise_acts(a, first_pass, values):
+            passes = values.shape[1]
+            nc.vector.quantize_mx(
+                out=a_codes[:, a, first_pass : first_pass + passes, :]
+                .rearrange("p s n -> p (s n)")
+                .bitcast(E5M2X4),
+                scales=a_scales[:, a, first_pass : first_pass + passes, :].rearrange("p s n -> p (s n)"),
+                in_=values.rearrange("p s n t -> p (s n t)"),
+            )
+
+        def gate_gradients(a, gate_inputs):
+            iou_sb, c_sb, g_sb = gate_inputs
+            ti = tanh_of(iou_sb[:, 0:HID], 0.5, xs, "ti")
+            to = tanh_of(iou_sb[:, HID : 2 * HID], 0.5, xs, "to")
+            tcc = tanh_of(c_sb[:, :], 1.0, xs, "tcc")
+            tu = tanh_of(iou_sb[:, 2 * HID : 3 * HID], 1.0, xs, "tu")
+            sqc = square_of(tcc, 1.0, xs, "sqc")
+            squ = square_of(tu, 0.5, xs, "squ")
+            g_bank = tp16.tile([P, 2, PACK, P], BF16, name="bank16")
+            transpose_512(g_bank[:, 0], g_sb[:, 0, :], ident16)
+            transpose_512(g_bank[:, 1], g_sb[:, 1, :], ident16)
+            gh = by_node(g_bank[:, 0])
+            gc = by_node(g_bank[:, 1])
+
+            diou = bfp.tile([P, GATES, P, PACK], BF16, name="diou", align_bytes=64)
+            gho = xv.tile([P, P, PACK], F32, name="gho")
+            fused(gho[:], to[:], 1.0, ALU.add, gh, ALU.mult)
+            back = xv.tile([P, P, PACK], F32, name="back")
+            fused(back[:], sqc[:], -1.0, ALU.add, gho[:], ALU.mult)
+            m2dc = xs.tile([P, P, PACK], F32, name="m2dc")
+            fused(m2dc[:], gc, -2.0, ALU.mult, back[:], ALU.add)
+            oo = xv.tile([P, P, PACK], F32, name="oo")
+            fused(oo[:], to[:], -1.0, ALU.add, gho[:], ALU.mult)
+            fused(diou[:, 1], oo[:], -0.25, ALU.mult, tcc[:], ALU.mult)
+            dsi = xv.tile([P, P, PACK], F32, name="dsi")
+            fused(dsi[:], ti[:], 1.0, ALU.add, m2dc[:], ALU.mult)
+            fused(diou[:, 2], squ[:], -0.25, ALU.add, dsi[:], ALU.mult)
+            ii = xv.tile([P, P, PACK], F32, name="ii")
+            fused(ii[:], ti[:], -1.0, ALU.add, dsi[:], ALU.mult)
+            fused(diou[:, 0], ii[:], 0.125, ALU.mult, tu[:], ALU.mult)
+            quantise_acts(a, 1, diou[:, 1:3])
+            quantise_acts(a, 0, diou[:, 0:1])
+            return m2dc
+
+        def forget_gradient(a, d, forget_inputs, nc_bank, m2dc):
+            fl_sb = forget_inputs[0]
+            tf = tanh_of(fl_sb[:, d * HID : (d + 1) * HID], 0.5, fs, "tf")
+            sqf = square_of(tf, 0.5, fs, "sqf")
+            dcn = fs.tile([P, P, PACK], F32, name="dcn")
+            fused(dcn[:], by_node(nc_bank), 0.5, ALU.mult, m2dc[:], ALU.mult)
+            df = bfp.tile([P, 1, P, PACK], BF16, name="df", align_bytes=64)
+            fused(df[:, 0], sqf[:], -0.25, ALU.add, dcn[:], ALU.mult)
+            quantise_acts(a, GATES + d, df[:])
+
+        def multiply(a, d):
+            acc = accp.tile([P, HID], F32, name="acc")
+            pairs = [(g, 1 + g) for g in range(GATES)] + [(GATES + d, 0)]
+            for j, (a_pass, w_chunk) in enumerate(pairs):
+                nc.tensor.matmul_mx(
+                    out=acc[:],
+                    lhsT=a_codes[:, a, a_pass, :].bitcast(E5M2X4),
+                    lhsT_scale=a_scales[:, a, a_pass, :],
+                    rhs=w_codes[:, d, w_chunk, :].bitcast(E4M3X4),
+                    rhs_scale=w_scales[:, d, w_chunk, :],
+                    start=(j == 0),
+                    stop=(j == len(pairs) - 1),
+                )
+            res = outp.tile([P, HID], F32, name="res")
+            nc.scalar.copy(out=res[:], in_=acc[:])
+            nc.sync.dma_start(out=out_v[a][:, d, :], in_=res[:])
+
+        w_next = load_weights(0)
+        gate_next = load_gate_inputs(0)
+        forget_next = load_forget_inputs(0)
+        quantise_weights(0, w_next)
+        for a in range(NODE_TILES):
+            gate_inputs, forget_inputs = gate_next, forget_next
+            if a + 1 < NODE_TILES:
+                w_next = load_weights(a + 1)
+                gate_next = load_gate_inputs(a + 1)
+                forget_next = load_forget_inputs(a + 1)
+            m2dc = gate_gradients(a, gate_inputs)
+            for d in range(CHILDREN):
+                if d % 2 == 0:
+                    nc_bank = tp16.tile([P, 2, PACK, P], BF16, name="bank16")
+                    for e in range(2):
+                        transpose_512(
+                            nc_bank[:, e], forget_inputs[1][:, (d + e) * HID : (d + e + 1) * HID], ident16
+                        )
+                forget_gradient(a, d, forget_inputs, nc_bank[:, d % 2], m2dc)
+                if d <= a:
+                    multiply(a, d)
+            if a + 1 < NODE_TILES:
+                quantise_weights(a + 1, w_next)
+                for earlier in range(a + 1):
+                    multiply(earlier, a + 1)

@@ -14,7 +14,6 @@ ALU = mybir.AluOpType
 
 P = 128
 PACK = 4
-K_PASS = P * PACK
 NODES = 512
 CHILDREN = 4
 HID = 512
@@ -24,6 +23,15 @@ W_CHUNKS = 1 + GATES
 A_PASSES = GATES + CHILDREN
 
 VECTOR_COLS = 192
+SQUARE_LEAD = 2
+TANH_LEAD = 3
+REGROUP_LEAD = 2
+T16_LEAD = 2
+OPEN_AHEAD = 1
+TP32_BANKS = 3
+TP16_BANKS = 2
+ACC_BANKS = 3
+LOAD_LEAD = 7
 
 FLOPS = 2 * NODES * CHILDREN * HID * (HID + GATES * HID)
 BYTES = (
@@ -54,15 +62,15 @@ def tile_generictreelstmcell_t_v_kernel(
         keep = ctx.enter_context(tc.tile_pool(name="keep", bufs=1))
         raw_a = ctx.enter_context(tc.tile_pool(name="raw_a", bufs=2))
         raw_w = ctx.enter_context(tc.tile_pool(name="raw_w", bufs=8))
-        grp = ctx.enter_context(tc.tile_pool(name="grp", bufs=3))
+        grp = ctx.enter_context(tc.tile_pool(name="grp", bufs=4))
         xs = ctx.enter_context(tc.tile_pool(name="xs", bufs=2))
         xv = ctx.enter_context(tc.tile_pool(name="xv", bufs=1))
-        fs = ctx.enter_context(tc.tile_pool(name="fs", bufs=3))
+        fs = ctx.enter_context(tc.tile_pool(name="fs", bufs=4))
         bfp = ctx.enter_context(tc.tile_pool(name="bfp", bufs=2))
         outp = ctx.enter_context(tc.tile_pool(name="outp", bufs=4))
-        tp32 = ctx.enter_context(tc.psum_pool(name="tp32", bufs=3))
-        tp16 = ctx.enter_context(tc.psum_pool(name="tp16", bufs=2))
-        accp = ctx.enter_context(tc.psum_pool(name="accp", bufs=3))
+        tp32 = ctx.enter_context(tc.psum_pool(name="tp32", bufs=TP32_BANKS))
+        tp16 = ctx.enter_context(tc.psum_pool(name="tp16", bufs=TP16_BANKS))
+        accp = ctx.enter_context(tc.psum_pool(name="accp", bufs=ACC_BANKS))
 
         ident32 = consts.tile([P, P], F32)
         make_identity(nc, ident32[:])
@@ -74,38 +82,33 @@ def tile_generictreelstmcell_t_v_kernel(
         a_codes = keep.tile([P, NODE_TILES, A_PASSES, P], U32, align_bytes=64)
         a_scales = keep.tile([P, NODE_TILES, A_PASSES, P], U8, align_bytes=64)
 
-        def load_weights(d):
-            chunks = []
-            for q in range(W_CHUNKS):
-                w_raw = raw_w.tile([P, PACK, HID], BF16, name="w_raw")
-                nc.sync.dma_start(out=w_raw[:], in_=uf_v[d] if q == 0 else ui_v[d, q - 1])
-                chunks.append(w_raw)
-            return chunks
+        def load_weight_chunk(d, q):
+            w_raw = raw_w.tile([P, PACK, HID], BF16, name="w_raw")
+            nc.sync.dma_start(out=w_raw[:], in_=uf_v[d] if q == 0 else ui_v[d, q - 1])
+            return w_raw
 
-        def quantise_weights(d, chunks):
-            for q in range(W_CHUNKS):
-                grouped = grp.tile([P, HID, PACK], BF16, name="grouped", align_bytes=64)
-                for engine_copy, h0, h1 in (
-                    (nc.vector.tensor_copy, 0, VECTOR_COLS),
-                    (nc.scalar.copy, VECTOR_COLS, HID),
-                ):
-                    engine_copy(
-                        out=grouped[:, h0:h1, :].rearrange("p (c i) t -> p c t i", i=4),
-                        in_=chunks[q][:, :, h0:h1].rearrange("p t (c i) -> p c t i", i=4),
-                    )
-                nc.vector.quantize_mx(
-                    out=w_codes[:, d, q, :].bitcast(E4M3X4),
-                    scales=w_scales[:, d, q, :],
-                    in_=grouped[:].rearrange("p h t -> p (h t)"),
-                )
+        def regroup(engine_copy, grouped, w_raw, h0, h1):
+            engine_copy(
+                out=grouped[:, h0:h1, :].rearrange("p (c i) t -> p c t i", i=4),
+                in_=w_raw[:, :, h0:h1].rearrange("p t (c i) -> p c t i", i=4),
+            )
+
+        def quantise_weight_chunk(d, q, grouped):
+            nc.vector.quantize_mx(
+                out=w_codes[:, d, q, :].bitcast(E4M3X4),
+                scales=w_scales[:, d, q, :],
+                in_=grouped[:].rearrange("p h t -> p (h t)"),
+            )
 
         def load_gate_inputs(a):
-            iou_sb = raw_a.tile([P, GATES * HID], F32, name="iou_sb")
-            nc.sync.dma_start(out=iou_sb[:], in_=iou_v[a])
+            iou_sb = raw_a.tile([P, GATES, HID], F32, name="iou_sb")
             c_sb = raw_a.tile([P, HID], F32, name="c_sb")
-            nc.sync.dma_start(out=c_sb[:], in_=c_v[a])
             g_sb = raw_a.tile([P, 2, HID], BF16, name="g_sb")
+            nc.sync.dma_start(out=iou_sb[:, 1, :], in_=iou_v[a][:, HID : 2 * HID])
             nc.sync.dma_start(out=g_sb[:], in_=g_v[a])
+            nc.sync.dma_start(out=c_sb[:], in_=c_v[a])
+            nc.sync.dma_start(out=iou_sb[:, 0, :], in_=iou_v[a][:, 0:HID])
+            nc.sync.dma_start(out=iou_sb[:, 2, :], in_=iou_v[a][:, 2 * HID : 3 * HID])
             return iou_sb, c_sb, g_sb
 
         def load_forget_inputs(a):
@@ -119,12 +122,15 @@ def tile_generictreelstmcell_t_v_kernel(
             for t in range(PACK):
                 nc.tensor.transpose(bank[:, t, :], src[:, t * P : (t + 1) * P], ident[:])
 
+        def transposed32(src):
+            bank = tp32.tile([P, PACK, P], F32, name="bank32")
+            transpose_512(bank, src, ident32)
+            return bank
+
         def by_node(bank):
             return bank.rearrange("p t n -> p n t")
 
-        def tanh_of(src, scale, pool, name):
-            bank = tp32.tile([P, PACK, P], F32, name="bank32")
-            transpose_512(bank, src, ident32)
+        def tanh_of(bank, scale, pool, name):
             res = pool.tile([P, P, PACK], F32, name=name)
             nc.scalar.activation(out=res[:], in_=by_node(bank[:]), func=ACT.Tanh, scale=scale)
             return res
@@ -147,89 +153,189 @@ def tile_generictreelstmcell_t_v_kernel(
                 in_=values.rearrange("p s n t -> p (s n t)"),
             )
 
-        def gate_gradients(a, gate_inputs):
-            iou_sb, c_sb, g_sb = gate_inputs
-            ti = tanh_of(iou_sb[:, 0:HID], 0.5, xs, "ti")
-            to = tanh_of(iou_sb[:, HID : 2 * HID], 0.5, xs, "to")
-            tcc = tanh_of(c_sb[:, :], 1.0, xs, "tcc")
-            tu = tanh_of(iou_sb[:, 2 * HID : 3 * HID], 1.0, xs, "tu")
-            sqc = square_of(tcc, 1.0, xs, "sqc")
-            squ = square_of(tu, 0.5, xs, "squ")
-            g_bank = tp16.tile([P, 2, PACK, P], BF16, name="bank16")
-            transpose_512(g_bank[:, 0], g_sb[:, 0, :], ident16)
-            transpose_512(g_bank[:, 1], g_sb[:, 1, :], ident16)
-            gh = by_node(g_bank[:, 0])
-            gc = by_node(g_bank[:, 1])
+        def mx_pass(acc, a, a_pass, d, w_chunk, start, stop):
+            nc.tensor.matmul_mx(
+                out=acc[:],
+                lhsT=a_codes[:, a, a_pass, :].bitcast(E5M2X4),
+                lhsT_scale=a_scales[:, a, a_pass, :],
+                rhs=w_codes[:, d, w_chunk, :].bitcast(E4M3X4),
+                rhs_scale=w_scales[:, d, w_chunk, :],
+                start=start,
+                stop=stop,
+            )
 
-            diou = bfp.tile([P, GATES, P, PACK], BF16, name="diou", align_bytes=64)
-            gho = xv.tile([P, P, PACK], F32, name="gho")
-            fused(gho[:], to[:], 1.0, ALU.add, gh, ALU.mult)
-            back = xv.tile([P, P, PACK], F32, name="back")
-            fused(back[:], sqc[:], -1.0, ALU.add, gho[:], ALU.mult)
-            m2dc = xs.tile([P, P, PACK], F32, name="m2dc")
-            fused(m2dc[:], gc, -2.0, ALU.mult, back[:], ALU.add)
-            oo = xv.tile([P, P, PACK], F32, name="oo")
-            fused(oo[:], to[:], -1.0, ALU.add, gho[:], ALU.mult)
-            fused(diou[:, 1], oo[:], -0.25, ALU.mult, tcc[:], ALU.mult)
-            dsi = xv.tile([P, P, PACK], F32, name="dsi")
-            fused(dsi[:], ti[:], 1.0, ALU.add, m2dc[:], ALU.mult)
-            fused(diou[:, 2], squ[:], -0.25, ALU.add, dsi[:], ALU.mult)
-            ii = xv.tile([P, P, PACK], F32, name="ii")
-            fused(ii[:], ti[:], -1.0, ALU.add, dsi[:], ALU.mult)
-            fused(diou[:, 0], ii[:], 0.125, ALU.mult, tu[:], ALU.mult)
-            quantise_acts(a, 1, diou[:, 1:3])
-            quantise_acts(a, 0, diou[:, 0:1])
-            return m2dc
-
-        def forget_gradient(a, d, forget_inputs, nc_bank, m2dc):
-            fl_sb = forget_inputs[0]
-            tf = tanh_of(fl_sb[:, d * HID : (d + 1) * HID], 0.5, fs, "tf")
-            sqf = square_of(tf, 0.5, fs, "sqf")
-            dcn = fs.tile([P, P, PACK], F32, name="dcn")
-            fused(dcn[:], by_node(nc_bank), 0.5, ALU.mult, m2dc[:], ALU.mult)
-            df = bfp.tile([P, 1, P, PACK], BF16, name="df", align_bytes=64)
-            fused(df[:, 0], sqf[:], -0.25, ALU.add, dcn[:], ALU.mult)
-            quantise_acts(a, GATES + d, df[:])
-
-        def multiply(a, d):
+        def open_block(a, d):
             acc = accp.tile([P, HID], F32, name="acc")
-            pairs = [(g, 1 + g) for g in range(GATES)] + [(GATES + d, 0)]
-            for j, (a_pass, w_chunk) in enumerate(pairs):
-                nc.tensor.matmul_mx(
-                    out=acc[:],
-                    lhsT=a_codes[:, a, a_pass, :].bitcast(E5M2X4),
-                    lhsT_scale=a_scales[:, a, a_pass, :],
-                    rhs=w_codes[:, d, w_chunk, :].bitcast(E4M3X4),
-                    rhs_scale=w_scales[:, d, w_chunk, :],
-                    start=(j == 0),
-                    stop=(j == len(pairs) - 1),
-                )
+            for g in range(GATES):
+                mx_pass(acc, a, g, d, 1 + g, g == 0, False)
+            return acc
+
+        def close_block(a, d, acc):
+            mx_pass(acc, a, GATES + d, d, 0, False, True)
+
+        def store(a, d, acc):
             res = outp.tile([P, HID], F32, name="res")
             nc.scalar.copy(out=res[:], in_=acc[:])
             nc.sync.dma_start(out=out_v[a][:, d, :], in_=res[:])
 
-        w_next = load_weights(0)
-        gate_next = load_gate_inputs(0)
-        forget_next = load_forget_inputs(0)
-        quantise_weights(0, w_next)
+        chunks = [(d, q) for d in range(CHILDREN) for q in range(W_CHUNKS)]
+        steps = []
         for a in range(NODE_TILES):
-            gate_inputs, forget_inputs = gate_next, forget_next
-            if a + 1 < NODE_TILES:
-                w_next = load_weights(a + 1)
-                gate_next = load_gate_inputs(a + 1)
-                forget_next = load_forget_inputs(a + 1)
-            m2dc = gate_gradients(a, gate_inputs)
-            for d in range(CHILDREN):
-                if d % 2 == 0:
-                    nc_bank = tp16.tile([P, 2, PACK, P], BF16, name="bank16")
-                    for e in range(2):
-                        transpose_512(
-                            nc_bank[:, e], forget_inputs[1][:, (d + e) * HID : (d + e + 1) * HID], ident16
-                        )
-                forget_gradient(a, d, forget_inputs, nc_bank[:, d % 2], m2dc)
-                if d <= a:
-                    multiply(a, d)
-            if a + 1 < NODE_TILES:
-                quantise_weights(a + 1, w_next)
-                for earlier in range(a + 1):
-                    multiply(earlier, a + 1)
+            steps.append((a, None))
+            steps.extend([(a, d) for d in range(CHILDREN)])
+        n_steps = len(steps)
+        step_of = dict((steps[i], i) for i in range(n_steps))
+
+        def chunk_of(i):
+            return chunks[i] if 0 <= i < len(chunks) else None
+
+        def is_gate_step(i):
+            return 0 <= i < n_steps and steps[i][1] is None
+
+        def is_child_step(i):
+            return 0 <= i < n_steps and steps[i][1] is not None
+
+        blocks = [(a, d) for a in range(NODE_TILES) for d in range(CHILDREN)]
+        close_round = dict(
+            ((a, d), max(step_of[a, d] + 1, chunks.index((d, W_CHUNKS - 1)))) for a, d in blocks
+        )
+        open_round = dict(
+            ((a, d), max(step_of[a, None], chunks.index((d, W_CHUNKS - 1)), close_round[a, d] - OPEN_AHEAD))
+            for a, d in blocks
+        )
+
+        raw_gate = {}
+        raw_forget = {}
+        raw_chunk = {}
+        bank_of = {}
+        tanh_out = {}
+        square_out = {}
+        grouped_of = {}
+        m2dc_of = {}
+        dcn_of = {}
+        acc_of = {}
+        df_of = {}
+
+        def loads(i):
+            if is_gate_step(i):
+                raw_gate[i] = load_gate_inputs(steps[i][0])
+            if is_child_step(i) and steps[i][1] == 0:
+                raw_forget[steps[i][0]] = load_forget_inputs(steps[i][0])
+            if chunk_of(i) is not None:
+                raw_chunk[i] = load_weight_chunk(chunk_of(i)[0], chunk_of(i)[1])
+
+        def transposes16(i):
+            if is_child_step(i) and steps[i][1] % 2 == 0:
+                a, d = steps[i]
+                nc_bank = tp16.tile([P, 2, PACK, P], BF16, name="bank16")
+                for e in range(2):
+                    transpose_512(nc_bank[:, e], raw_forget[a][1][:, (d + e) * HID : (d + e + 1) * HID], ident16)
+                    bank_of["nc", i + e] = nc_bank[:, e]
+
+        def tanh_part(i):
+            if is_gate_step(i):
+                iou_sb, c_sb, g_sb = raw_gate[i]
+                tanh_out["o", i] = tanh_of(transposed32(iou_sb[:, 1, :]), 0.5, xs, "to")
+                g_bank = tp16.tile([P, 2, PACK, P], BF16, name="bank16")
+                for e in range(2):
+                    transpose_512(g_bank[:, e], g_sb[:, e, :], ident16)
+                bank_of["gh", i] = g_bank[:, 0]
+                bank_of["gc", i] = g_bank[:, 1]
+                tanh_out["c", i] = tanh_of(transposed32(c_sb[:, :]), 1.0, xs, "tcc")
+                tanh_out["i", i] = tanh_of(transposed32(iou_sb[:, 0, :]), 0.5, xs, "ti")
+                square_out["c", i] = square_of(tanh_out["c", i], 1.0, xs, "sqc")
+                tanh_out["u", i] = tanh_of(transposed32(iou_sb[:, 2, :]), 1.0, xs, "tu")
+            if is_child_step(i):
+                a, d = steps[i]
+                fl_bank = transposed32(raw_forget[a][0][:, d * HID : (d + 1) * HID])
+                tanh_out["f", i] = tanh_of(fl_bank, 0.5, fs, "tf")
+
+        def square_part(i):
+            if is_gate_step(i):
+                square_out["u", i] = square_of(tanh_out["u", i], 0.5, xs, "squ")
+            if is_child_step(i):
+                square_out["f", i] = square_of(tanh_out["f", i], 0.5, fs, "sqf")
+
+        def scalar_regroup(i):
+            if chunk_of(i) is not None:
+                grouped_of[i] = grp.tile([P, HID, PACK], BF16, name="grouped", align_bytes=64)
+                regroup(nc.scalar.copy, grouped_of[i], raw_chunk[i], VECTOR_COLS, HID)
+
+        def vector_regroup(i):
+            if chunk_of(i) is not None:
+                regroup(nc.vector.tensor_copy, grouped_of[i], raw_chunk[i], 0, VECTOR_COLS)
+
+        def vector_quantise_chunk(i):
+            if chunk_of(i) is not None:
+                quantise_weight_chunk(chunk_of(i)[0], chunk_of(i)[1], grouped_of[i])
+
+        def vector_next_dcn(i):
+            if is_child_step(i):
+                dcn_of[i] = fs.tile([P, P, PACK], F32, name="dcn")
+                fused(dcn_of[i][:], by_node(bank_of["nc", i]), 0.5, ALU.mult, m2dc_of[steps[i][0]][:], ALU.mult)
+
+        def vector_quantise_child(i):
+            if is_child_step(i):
+                quantise_acts(steps[i][0], GATES + steps[i][1], df_of[i][:])
+
+        def vector_gate_step(i):
+            a = steps[i][0]
+            to, tcc, ti, tu = tanh_out["o", i], tanh_out["c", i], tanh_out["i", i], tanh_out["u", i]
+            diou = bfp.tile([P, GATES, P, PACK], BF16, name="diou", align_bytes=64)
+            gho = xv.tile([P, P, PACK], F32, name="gho")
+            back = xv.tile([P, P, PACK], F32, name="back")
+            m2dc = xs.tile([P, P, PACK], F32, name="m2dc")
+            oo = xv.tile([P, P, PACK], F32, name="oo")
+            dsi = xv.tile([P, P, PACK], F32, name="dsi")
+            ii = xv.tile([P, P, PACK], F32, name="ii")
+            m2dc_of[a] = m2dc
+            fused(gho[:], to[:], 1.0, ALU.add, by_node(bank_of["gh", i]), ALU.mult)
+            vector_quantise_child(i - 1)
+            if i == 0:
+                vector_regroup(0)
+            fused(back[:], square_out["c", i][:], -1.0, ALU.add, gho[:], ALU.mult)
+            fused(oo[:], to[:], -1.0, ALU.add, gho[:], ALU.mult)
+            fused(m2dc[:], by_node(bank_of["gc", i]), -2.0, ALU.mult, back[:], ALU.add)
+            fused(diou[:, 1], oo[:], -0.25, ALU.mult, tcc[:], ALU.mult)
+            fused(dsi[:], ti[:], 1.0, ALU.add, m2dc[:], ALU.mult)
+            vector_quantise_chunk(i)
+            fused(diou[:, 2], square_out["u", i][:], -0.25, ALU.add, dsi[:], ALU.mult)
+            fused(ii[:], ti[:], -1.0, ALU.add, dsi[:], ALU.mult)
+            vector_next_dcn(i + 1)
+            fused(diou[:, 0], ii[:], 0.125, ALU.mult, tu[:], ALU.mult)
+            vector_regroup(i + 1)
+            quantise_acts(a, 1, diou[:, 1:3])
+            quantise_acts(a, 0, diou[:, 0:1])
+
+        def vector_child_step(i):
+            vector_next_dcn(i + 1)
+            df_of[i] = bfp.tile([P, 1, P, PACK], BF16, name="df", align_bytes=64)
+            fused(df_of[i][:, 0], square_out["f", i][:], -0.25, ALU.add, dcn_of[i][:], ALU.mult)
+            vector_quantise_child(i - 1)
+            vector_regroup(i + 1)
+            vector_quantise_chunk(i)
+
+        with tc.manual_schedule():
+            for i in range(-LOAD_LEAD, n_steps + 2):
+                loads(i + LOAD_LEAD)
+                scalar_regroup(i + REGROUP_LEAD)
+                for a, d in blocks:
+                    if close_round[a, d] + 1 == i:
+                        store(a, d, acc_of[a, d])
+                square_part(i + SQUARE_LEAD)
+                transposes16(i + T16_LEAD)
+                tanh_part(i + TANH_LEAD)
+                if is_gate_step(i):
+                    vector_gate_step(i)
+                if is_child_step(i):
+                    vector_child_step(i)
+                if i == n_steps:
+                    vector_quantise_child(i - 1)
+                for a, d in blocks:
+                    if close_round[a, d] == i and open_round[a, d] < i:
+                        close_block(a, d, acc_of[a, d])
+                for a, d in blocks:
+                    if open_round[a, d] == i:
+                        acc_of[a, d] = open_block(a, d)
+                        if close_round[a, d] == i:
+                            close_block(a, d, acc_of[a, d])

@@ -20,14 +20,14 @@ HID = 512
 NODE_TILES = NODES // P
 GATES = 3
 W_CHUNKS = 1 + GATES
+STEPS_PER_TILE = 1 + CHILDREN
 A_PASSES = GATES + CHILDREN
 
-VECTOR_COLS = 192
+VECTOR_COLS = 224
 SQUARE_LEAD = 2
 TANH_LEAD = 3
 REGROUP_LEAD = 2
 T16_LEAD = 2
-OPEN_AHEAD = 1
 TP32_BANKS = 3
 TP16_BANKS = 2
 ACC_BANKS = 3
@@ -61,6 +61,7 @@ def tile_generictreelstmcell_t_v_kernel(
         consts = ctx.enter_context(tc.tile_pool(name="consts", bufs=1))
         keep = ctx.enter_context(tc.tile_pool(name="keep", bufs=1))
         raw_a = ctx.enter_context(tc.tile_pool(name="raw_a", bufs=2))
+        raw_f = ctx.enter_context(tc.tile_pool(name="raw_f", bufs=4))
         raw_w = ctx.enter_context(tc.tile_pool(name="raw_w", bufs=8))
         grp = ctx.enter_context(tc.tile_pool(name="grp", bufs=4))
         xs = ctx.enter_context(tc.tile_pool(name="xs", bufs=2))
@@ -111,11 +112,12 @@ def tile_generictreelstmcell_t_v_kernel(
             nc.sync.dma_start(out=iou_sb[:, 2, :], in_=iou_v[a][:, 2 * HID : 3 * HID])
             return iou_sb, c_sb, g_sb
 
-        def load_forget_inputs(a):
-            fl_sb = raw_a.tile([P, CHILDREN * HID], F32, name="fl_sb")
-            nc.sync.dma_start(out=fl_sb[:], in_=fl_v[a])
-            nc_sb = raw_a.tile([P, CHILDREN * HID], BF16, name="nc_sb")
-            nc.sync.dma_start(out=nc_sb[:], in_=nc_v[a])
+        def load_forget_inputs(a, d):
+            cols = slice(d * HID, (d + 2) * HID)
+            fl_sb = raw_f.tile([P, 2 * HID], F32, name="fl_sb")
+            nc.sync.dma_start(out=fl_sb[:], in_=fl_v[a][:, cols])
+            nc_sb = raw_f.tile([P, 2 * HID], BF16, name="nc_sb")
+            nc.sync.dma_start(out=nc_sb[:], in_=nc_v[a][:, cols])
             return fl_sb, nc_sb
 
         def transpose_512(bank, src, ident):
@@ -187,7 +189,7 @@ def tile_generictreelstmcell_t_v_kernel(
         step_of = dict((steps[i], i) for i in range(n_steps))
 
         def chunk_of(i):
-            return chunks[i] if 0 <= i < len(chunks) else None
+            return chunks[i + 1] if 0 <= i + 1 < len(chunks) else None
 
         def is_gate_step(i):
             return 0 <= i < n_steps and steps[i][1] is None
@@ -196,13 +198,16 @@ def tile_generictreelstmcell_t_v_kernel(
             return 0 <= i < n_steps and steps[i][1] is not None
 
         blocks = [(a, d) for a in range(NODE_TILES) for d in range(CHILDREN)]
-        close_round = dict(
-            ((a, d), max(step_of[a, d] + 1, chunks.index((d, W_CHUNKS - 1)))) for a, d in blocks
-        )
-        open_round = dict(
-            ((a, d), max(step_of[a, None], chunks.index((d, W_CHUNKS - 1)), close_round[a, d] - OPEN_AHEAD))
-            for a, d in blocks
-        )
+        close_round = {}
+        open_round = {}
+        for a, d in blocks:
+            weights_ready = chunks.index((d, W_CHUNKS - 1)) - 1
+            if step_of[a, d] + 1 >= weights_ready:
+                close_round[a, d] = step_of[a, d] + 1
+                open_round[a, d] = max(step_of[a, None], weights_ready, close_round[a, d] - 1)
+            else:
+                close_round[a, d] = -(-weights_ready // STEPS_PER_TILE) * STEPS_PER_TILE
+                open_round[a, d] = close_round[a, d]
 
         raw_gate = {}
         raw_forget = {}
@@ -219,17 +224,17 @@ def tile_generictreelstmcell_t_v_kernel(
         def loads(i):
             if is_gate_step(i):
                 raw_gate[i] = load_gate_inputs(steps[i][0])
-            if is_child_step(i) and steps[i][1] == 0:
-                raw_forget[steps[i][0]] = load_forget_inputs(steps[i][0])
+            if is_child_step(i) and steps[i][1] % 2 == 0:
+                raw_forget[i] = load_forget_inputs(steps[i][0], steps[i][1])
+                raw_forget[i + 1] = raw_forget[i]
             if chunk_of(i) is not None:
                 raw_chunk[i] = load_weight_chunk(chunk_of(i)[0], chunk_of(i)[1])
 
         def transposes16(i):
             if is_child_step(i) and steps[i][1] % 2 == 0:
-                a, d = steps[i]
                 nc_bank = tp16.tile([P, 2, PACK, P], BF16, name="bank16")
                 for e in range(2):
-                    transpose_512(nc_bank[:, e], raw_forget[a][1][:, (d + e) * HID : (d + e + 1) * HID], ident16)
+                    transpose_512(nc_bank[:, e], raw_forget[i][1][:, e * HID : (e + 1) * HID], ident16)
                     bank_of["nc", i + e] = nc_bank[:, e]
 
         def tanh_part(i):
@@ -246,8 +251,8 @@ def tile_generictreelstmcell_t_v_kernel(
                 square_out["c", i] = square_of(tanh_out["c", i], 1.0, xs, "sqc")
                 tanh_out["u", i] = tanh_of(transposed32(iou_sb[:, 2, :]), 1.0, xs, "tu")
             if is_child_step(i):
-                a, d = steps[i]
-                fl_bank = transposed32(raw_forget[a][0][:, d * HID : (d + 1) * HID])
+                e = steps[i][1] % 2
+                fl_bank = transposed32(raw_forget[i][0][:, e * HID : (e + 1) * HID])
                 tanh_out["f", i] = tanh_of(fl_bank, 0.5, fs, "tf")
 
         def square_part(i):
@@ -291,19 +296,19 @@ def tile_generictreelstmcell_t_v_kernel(
             m2dc_of[a] = m2dc
             fused(gho[:], to[:], 1.0, ALU.add, by_node(bank_of["gh", i]), ALU.mult)
             vector_quantise_child(i - 1)
+            fused(oo[:], to[:], -1.0, ALU.add, gho[:], ALU.mult)
+            fused(back[:], square_out["c", i][:], -1.0, ALU.add, gho[:], ALU.mult)
+            fused(diou[:, 1], oo[:], -0.25, ALU.mult, tcc[:], ALU.mult)
             if i == 0:
                 vector_regroup(0)
-            fused(back[:], square_out["c", i][:], -1.0, ALU.add, gho[:], ALU.mult)
-            fused(oo[:], to[:], -1.0, ALU.add, gho[:], ALU.mult)
             fused(m2dc[:], by_node(bank_of["gc", i]), -2.0, ALU.mult, back[:], ALU.add)
-            fused(diou[:, 1], oo[:], -0.25, ALU.mult, tcc[:], ALU.mult)
-            fused(dsi[:], ti[:], 1.0, ALU.add, m2dc[:], ALU.mult)
             vector_quantise_chunk(i)
+            fused(dsi[:], ti[:], 1.0, ALU.add, m2dc[:], ALU.mult)
+            vector_next_dcn(i + 1)
             fused(diou[:, 2], square_out["u", i][:], -0.25, ALU.add, dsi[:], ALU.mult)
             fused(ii[:], ti[:], -1.0, ALU.add, dsi[:], ALU.mult)
-            vector_next_dcn(i + 1)
-            fused(diou[:, 0], ii[:], 0.125, ALU.mult, tu[:], ALU.mult)
             vector_regroup(i + 1)
+            fused(diou[:, 0], ii[:], 0.125, ALU.mult, tu[:], ALU.mult)
             quantise_acts(a, 1, diou[:, 1:3])
             quantise_acts(a, 0, diou[:, 0:1])
 
@@ -316,7 +321,7 @@ def tile_generictreelstmcell_t_v_kernel(
             vector_quantise_chunk(i)
 
         with tc.manual_schedule():
-            for i in range(-LOAD_LEAD, n_steps + 2):
+            for i in range(-LOAD_LEAD - 1, n_steps + 2):
                 loads(i + LOAD_LEAD)
                 scalar_regroup(i + REGROUP_LEAD)
                 for a, d in blocks:
@@ -325,6 +330,9 @@ def tile_generictreelstmcell_t_v_kernel(
                 square_part(i + SQUARE_LEAD)
                 transposes16(i + T16_LEAD)
                 tanh_part(i + TANH_LEAD)
+                if i == -1:
+                    vector_regroup(i)
+                    vector_quantise_chunk(i)
                 if is_gate_step(i):
                     vector_gate_step(i)
                 if is_child_step(i):
@@ -332,10 +340,8 @@ def tile_generictreelstmcell_t_v_kernel(
                 if i == n_steps:
                     vector_quantise_child(i - 1)
                 for a, d in blocks:
-                    if close_round[a, d] == i and open_round[a, d] < i:
-                        close_block(a, d, acc_of[a, d])
-                for a, d in blocks:
                     if open_round[a, d] == i:
                         acc_of[a, d] = open_block(a, d)
-                        if close_round[a, d] == i:
-                            close_block(a, d, acc_of[a, d])
+                for a, d in blocks:
+                    if close_round[a, d] == i:
+                        close_block(a, d, acc_of[a, d])

@@ -31,7 +31,7 @@ T16_LEAD = 2
 TP32_BANKS = 3
 TP16_BANKS = 2
 ACC_BANKS = 3
-LOAD_LEAD = 7
+LOAD_LEAD = 5
 
 FLOPS = 2 * NODES * CHILDREN * HID * (HID + GATES * HID)
 BYTES = (
@@ -62,8 +62,8 @@ def tile_generictreelstmcell_t_v_kernel(
         keep = ctx.enter_context(tc.tile_pool(name="keep", bufs=1))
         raw_a = ctx.enter_context(tc.tile_pool(name="raw_a", bufs=2))
         raw_f = ctx.enter_context(tc.tile_pool(name="raw_f", bufs=4))
-        raw_w = ctx.enter_context(tc.tile_pool(name="raw_w", bufs=8))
-        grp = ctx.enter_context(tc.tile_pool(name="grp", bufs=4))
+        raw_w = ctx.enter_context(tc.tile_pool(name="raw_w", bufs=6))
+        grp = ctx.enter_context(tc.tile_pool(name="grp", bufs=6))
         xs = ctx.enter_context(tc.tile_pool(name="xs", bufs=2))
         xv = ctx.enter_context(tc.tile_pool(name="xv", bufs=1))
         fs = ctx.enter_context(tc.tile_pool(name="fs", bufs=4))
@@ -314,9 +314,9 @@ def tile_generictreelstmcell_t_v_kernel(
 
         def vector_child_step(i):
             vector_next_dcn(i + 1)
+            vector_quantise_child(i - 1)
             df_of[i] = bfp.tile([P, 1, P, PACK], BF16, name="df", align_bytes=64)
             fused(df_of[i][:, 0], square_out["f", i][:], -0.25, ALU.add, dcn_of[i][:], ALU.mult)
-            vector_quantise_child(i - 1)
             vector_regroup(i + 1)
             vector_quantise_chunk(i)
 

@@ -90,8 +90,8 @@ def tile_generictreelstmcell_t_v_kernel(
 
         def regroup(engine_copy, grouped, w_raw, h0, h1):
             engine_copy(
-                out=grouped[:, h0:h1, :].rearrange("p (c i) t -> p c t i", i=4),
-                in_=w_raw[:, :, h0:h1].rearrange("p t (c i) -> p c t i", i=4),
+                out=grouped[:, h0:h1, :].rearrange("p (c i) t -> p c t i", i=8),
+                in_=w_raw[:, :, h0:h1].rearrange("p t (c i) -> p c t i", i=8),
             )
 
         def quantise_weight_chunk(d, q, grouped):

@@ -31,6 +31,7 @@ T16_LEAD = 2
 TP32_BANKS = 3
 TP16_BANKS = 2
 ACC_BANKS = 3
+WARM_FIRST = 4
 LOAD_LEAD = 5
 
 FLOPS = 2 * NODES * CHILDREN * HID * (HID + GATES * HID)
@@ -77,6 +78,14 @@ def tile_generictreelstmcell_t_v_kernel(
         make_identity(nc, ident32[:])
         ident16 = consts.tile([P, P], BF16)
         make_identity(nc, ident16[:])
+
+        ones = consts.tile([P, HID], BF16)
+        nc.vector.memset(ones[:], 1.0)
+        unread = accp.tile([P, HID], F32, name="acc")
+
+        def keep_clock_up(count):
+            for r in range(count):
+                nc.tensor.matmul(out=unread[:], lhsT=ident16[:], rhs=ones[:], start=True, stop=True)
 
         w_codes = keep.tile([P, CHILDREN, W_CHUNKS, HID], U32, align_bytes=64)
         w_scales = keep.tile([P, CHILDREN, W_CHUNKS, HID], U8, align_bytes=64)
@@ -127,6 +136,7 @@ def tile_generictreelstmcell_t_v_kernel(
         def transposed32(src):
             bank = tp32.tile([P, PACK, P], F32, name="bank32")
             transpose_512(bank, src, ident32)
+            keep_clock_up(warm["count"])
             return bank
 
         def by_node(bank):
@@ -209,6 +219,7 @@ def tile_generictreelstmcell_t_v_kernel(
                 close_round[a, d] = -(-weights_ready // STEPS_PER_TILE) * STEPS_PER_TILE
                 open_round[a, d] = close_round[a, d]
 
+        warm = {"count": 0}
         raw_gate = {}
         raw_forget = {}
         raw_chunk = {}
@@ -321,7 +332,9 @@ def tile_generictreelstmcell_t_v_kernel(
             vector_quantise_chunk(i)
 
         with tc.manual_schedule():
+            keep_clock_up(WARM_FIRST)
             for i in range(-LOAD_LEAD - 1, n_steps + 2):
+                warm["count"] = 0 if i >= min(open_round[block] for block in blocks) else (1 if i + TANH_LEAD <= 0 else 2)
                 loads(i + LOAD_LEAD)
                 scalar_regroup(i + REGROUP_LEAD)
                 for a, d in blocks:

from contextlib import ExitStack

import concourse.mybir as mybir
from concourse.masks import make_identity

F32 = mybir.dt.float32
BF16 = mybir.dt.bfloat16
U32 = mybir.dt.uint32
U8 = mybir.dt.uint8
E4M3X4 = mybir.dt.float8_e4m3fn_x4
E5M2X4 = mybir.dt.float8_e5m2_x4
ACT = mybir.ActivationFunctionType
ALU = mybir.AluOpType

P = 128
PACK = 4
NODES = 512
CHILDREN = 4
HID = 512
NODE_TILES = NODES // P
GATES = 3
W_CHUNKS = 1 + GATES
STEPS_PER_TILE = 1 + CHILDREN
A_PASSES = GATES + CHILDREN

VECTOR_COLS = 224
SQUARE_LEAD = 2
TANH_LEAD = 3
REGROUP_LEAD = 2
T16_LEAD = 2
TP32_BANKS = 3
TP16_BANKS = 2
ACC_BANKS = 3
WARM_FIRST = 4
LOAD_LEAD = 5

FLOPS = 2 * NODES * CHILDREN * HID * (HID + GATES * HID)
BYTES = (
    2 * NODES * CHILDREN * HID
    + 2 * CHILDREN * (1 + GATES) * HID * HID
    + 4 * NODES * (CHILDREN + GATES + 1) * HID
    + 2 * 2 * NODES * HID
    + 4 * NODES * CHILDREN * HID
)


def tile_generictreelstmcell_t_v_kernel(
    tc, neighbour_h, neighbour_c, f_input, iou_input, U_f, U_iou, f_logits, iou, c, grad_out, out
):
    nc = tc.nc

    fl_v = f_logits.rearrange("(a p) d k -> a p (d k)", p=P)
    nc_v = neighbour_c.rearrange("(a p) d k -> a p (d k)", p=P)
    iou_v = iou.rearrange("(a p) j -> a p j", p=P)
    c_v = c.rearrange("(a p) k -> a p k", p=P)
    g_v = grad_out.rearrange("g (a p) k -> a p g k", p=P)
    out_v = out.rearrange("(a p) d h -> a p d h", p=P)
    uf_v = U_f.rearrange("d (t p) h -> d p t h", p=P)
    ui_v = U_iou.rearrange("d (g t p) h -> d g p t h", p=P, t=PACK)

    with ExitStack() as ctx:
        consts = ctx.enter_context(tc.tile_pool(name="consts", bufs=1))
        keep = ctx.enter_context(tc.tile_pool(name="keep", bufs=1))
        raw_a = ctx.enter_context(tc.tile_pool(name="raw_a", bufs=2))
        raw_f = ctx.enter_context(tc.tile_pool(name="raw_f", bufs=4))
        raw_w = ctx.enter_context(tc.tile_pool(name="raw_w", bufs=6))
        grp = ctx.enter_context(tc.tile_pool(name="grp", bufs=6))
        xs = ctx.enter_context(tc.tile_pool(name="xs", bufs=2))
        xv = ctx.enter_context(tc.tile_pool(name="xv", bufs=1))
        fs = ctx.enter_context(tc.tile_pool(name="fs", bufs=4))
        bfp = ctx.enter_context(tc.tile_pool(name="bfp", bufs=2))
        outp = ctx.enter_context(tc.tile_pool(name="outp", bufs=4))
        tp32 = ctx.enter_context(tc.psum_pool(name="tp32", bufs=TP32_BANKS))
        tp16 = ctx.enter_context(tc.psum_pool(name="tp16", bufs=TP16_BANKS))
        accp = ctx.enter_context(tc.psum_pool(name="accp", bufs=ACC_BANKS))

        ident32 = consts.tile([P, P], F32)
        make_identity(nc, ident32[:])
        ident16 = consts.tile([P, P], BF16)
        make_identity(nc, ident16[:])

        ones = consts.tile([P, HID], BF16)
        nc.vector.memset(ones[:], 1.0)
        unread = accp.tile([P, HID], F32, name="acc")

        def keep_clock_up(count):
            for r in range(count):
                nc.tensor.matmul(out=unread[:], lhsT=ident16[:], rhs=ones[:], start=True, stop=True)

        w_codes = keep.tile([P, CHILDREN, W_CHUNKS, HID], U32, align_bytes=64)
        w_scales = keep.tile([P, CHILDREN, W_CHUNKS, HID], U8, align_bytes=64)
        a_codes = keep.tile([P, NODE_TILES, A_PASSES, P], U32, align_bytes=64)
        a_scales = keep.tile([P, NODE_TILES, A_PASSES, P], U8, align_bytes=64)

        def load_weight_chunk(d, q):
            w_raw = raw_w.tile([P, PACK, HID], BF16, name="w_raw")
            nc.sync.dma_start(out=w_raw[:], in_=uf_v[d] if q == 0 else ui_v[d, q - 1])
            return w_raw

        def regroup(engine_copy, grouped, w_raw, h0, h1):
            engine_copy(
                out=grouped[:, h0:h1, :].rearrange("p (c i) t -> p c t i", i=8),
                in_=w_raw[:, :, h0:h1].rearrange("p t (c i) -> p c t i", i=8),
            )

        def quantise_weight_chunk(d, q, grouped):
            nc.vector.quantize_mx(
                out=w_codes[:, d, q, :].bitcast(E4M3X4),
                scales=w_scales[:, d, q, :],
                in_=grouped[:].rearrange("p h t -> p (h t)"),
            )

        def load_gate_inputs(a):
            iou_sb = raw_a.tile([P, GATES, HID], F32, name="iou_sb")
            c_sb = raw_a.tile([P, HID], F32, name="c_sb")
            g_sb = raw_a.tile([P, 2, HID], BF16, name="g_sb")
            nc.sync.dma_start(out=iou_sb[:, 1, :], in_=iou_v[a][:, HID : 2 * HID])
            nc.sync.dma_start(out=g_sb[:], in_=g_v[a])
            nc.sync.dma_start(out=c_sb[:], in_=c_v[a])
            nc.sync.dma_start(out=iou_sb[:, 0, :], in_=iou_v[a][:, 0:HID])
            nc.sync.dma_start(out=iou_sb[:, 2, :], in_=iou_v[a][:, 2 * HID : 3 * HID])
            return iou_sb, c_sb, g_sb

        def load_forget_inputs(a, d):
            cols = slice(d * HID, (d + 2) * HID)
            fl_sb = raw_f.tile([P, 2 * HID], F32, name="fl_sb")
            nc.sync.dma_start(out=fl_sb[:], in_=fl_v[a][:, cols])
            nc_sb = raw_f.tile([P, 2 * HID], BF16, name="nc_sb")
            nc.sync.dma_start(out=nc_sb[:], in_=nc_v[a][:, cols])
            return fl_sb, nc_sb

        def transpose_512(bank, src, ident):
            for t in range(PACK):
                nc.tensor.transpose(bank[:, t, :], src[:, t * P : (t + 1) * P], ident[:])

        def transposed32(src):
            bank = tp32.tile([P, PACK, P], F32, name="bank32")
            transpose_512(bank, src, ident32)
            keep_clock_up(warm["count"])
            return bank

        def by_node(bank):
            return bank.rearrange("p t n -> p n t")

        def tanh_of(bank, scale, pool, name):
            res = pool.tile([P, P, PACK], F32, name=name)
            nc.scalar.activation(out=res[:], in_=by_node(bank[:]), func=ACT.Tanh, scale=scale)
            return res

        def square_of(src, scale, pool, name):
            res = pool.tile([P, P, PACK], F32, name=name)
            nc.scalar.activation(out=res[:], in_=src[:], func=ACT.Square, scale=scale)
            return res

        def fused(out_ap, in0, scalar, op0, in1, op1):
            nc.vector.scalar_tensor_tensor(out=out_ap, in0=in0, scalar=scalar, in1=in1, op0=op0, op1=op1)

        def quantise_acts(a, first_pass, values):
            passes = values.shape[1]
            nc.vector.quantize_mx(
                out=a_codes[:, a, first_pass : first_pass + passes, :]
                .rearrange("p s n -> p (s n)")
                .bitcast(E5M2X4),
                scales=a_scales[:, a, first_pass : first_pass + passes, :].rearrange("p s n -> p (s n)"),
                in_=values.rearrange("p s n t -> p (s n t)"),
            )

        def mx_pass(acc, a, a_pass, d, w_chunk, start, stop):
            nc.tensor.matmul_mx(
                out=acc[:],
                lhsT=a_codes[:, a, a_pass, :].bitcast(E5M2X4),
                lhsT_scale=a_scales[:, a, a_pass, :],
                rhs=w_codes[:, d, w_chunk, :].bitcast(E4M3X4),
                rhs_scale=w_scales[:, d, w_chunk, :],
                start=start,
                stop=stop,
            )

        def open_block(a, d):
            acc = accp.tile([P, HID], F32, name="acc")
            for g in range(GATES):
                mx_pass(acc, a, g, d, 1 + g, g == 0, False)
            return acc

        def close_block(a, d, acc):
            mx_pass(acc, a, GATES + d, d, 0, False, True)

        def store(a, d, acc):
            res = outp.tile([P, HID], F32, name="res")
            nc.scalar.copy(out=res[:], in_=acc[:])
            nc.sync.dma_start(out=out_v[a][:, d, :], in_=res[:])

        chunks = [(d, q) for d in range(CHILDREN) for q in range(W_CHUNKS)]
        steps = []
        for a in range(NODE_TILES):
            steps.append((a, None))
            steps.extend([(a, d) for d in range(CHILDREN)])
        n_steps = len(steps)
        step_of = dict((steps[i], i) for i in range(n_steps))

        def chunk_of(i):
            return chunks[i + 1] if 0 <= i + 1 < len(chunks) else None

        def is_gate_step(i):
            return 0 <= i < n_steps and steps[i][1] is None

        def is_child_step(i):
            return 0 <= i < n_steps and steps[i][1] is not None

        blocks = [(a, d) for a in range(NODE_TILES) for d in range(CHILDREN)]
        close_round = {}
        open_round = {}
        for a, d in blocks:
            weights_ready = chunks.index((d, W_CHUNKS - 1)) - 1
            if step_of[a, d] + 1 >= weights_ready:
                close_round[a, d] = step_of[a, d] + 1
                open_round[a, d] = max(step_of[a, None], weights_ready, close_round[a, d] - 1)
            else:
                close_round[a, d] = -(-weights_ready // STEPS_PER_TILE) * STEPS_PER_TILE
                open_round[a, d] = close_round[a, d]

        warm = {"count": 0}
        raw_gate = {}
        raw_forget = {}
        raw_chunk = {}
        bank_of = {}
        tanh_out = {}
        square_out = {}
        grouped_of = {}
        m2dc_of = {}
        dcn_of = {}
        acc_of = {}
        df_of = {}

        def loads(i):
            if is_gate_step(i):
                raw_gate[i] = load_gate_inputs(steps[i][0])
            if is_child_step(i) and steps[i][1] % 2 == 0:
                raw_forget[i] = load_forget_inputs(steps[i][0], steps[i][1])
                raw_forget[i + 1] = raw_forget[i]
            if chunk_of(i) is not None:
                raw_chunk[i] = load_weight_chunk(chunk_of(i)[0], chunk_of(i)[1])

        def transposes16(i):
            if is_child_step(i) and steps[i][1] % 2 == 0:
                nc_bank = tp16.tile([P, 2, PACK, P], BF16, name="bank16")
                for e in range(2):
                    transpose_512(nc_bank[:, e], raw_forget[i][1][:, e * HID : (e + 1) * HID], ident16)
                    bank_of["nc", i + e] = nc_bank[:, e]

        def tanh_part(i):
            if is_gate_step(i):
                iou_sb, c_sb, g_sb = raw_gate[i]
                tanh_out["o", i] = tanh_of(transposed32(iou_sb[:, 1, :]), 0.5, xs, "to")
                g_bank = tp16.tile([P, 2, PACK, P], BF16, name="bank16")
                for e in range(2):
                    transpose_512(g_bank[:, e], g_sb[:, e, :], ident16)
                bank_of["gh", i] = g_bank[:, 0]
                bank_of["gc", i] = g_bank[:, 1]
                tanh_out["c", i] = tanh_of(transposed32(c_sb[:, :]), 1.0, xs, "tcc")
                tanh_out["i", i] = tanh_of(transposed32(iou_sb[:, 0, :]), 0.5, xs, "ti")
                square_out["c", i] = square_of(tanh_out["c", i], 1.0, xs, "sqc")
                tanh_out["u", i] = tanh_of(transposed32(iou_sb[:, 2, :]), 1.0, xs, "tu")
            if is_child_step(i):
                e = steps[i][1] % 2
                fl_bank = transposed32(raw_forget[i][0][:, e * HID : (e + 1) * HID])
                tanh_out["f", i] = tanh_of(fl_bank, 0.5, fs, "tf")

        def square_part(i):
            if is_gate_step(i):
                square_out["u", i] = square_of(tanh_out["u", i], 0.5, xs, "squ")
            if is_child_step(i):
                square_out["f", i] = square_of(tanh_out["f", i], 0.5, fs, "sqf")

        def scalar_regroup(i):
            if chunk_of(i) is not None:
                grouped_of[i] = grp.tile([P, HID, PACK], BF16, name="grouped", align_bytes=64)
                regroup(nc.scalar.copy, grouped_of[i], raw_chunk[i], VECTOR_COLS, HID)

        def vector_regroup(i):
            if chunk_of(i) is not None:
                regroup(nc.vector.tensor_copy, grouped_of[i], raw_chunk[i], 0, VECTOR_COLS)

        def vector_quantise_chunk(i):
            if chunk_of(i) is not None:
                quantise_weight_chunk(chunk_of(i)[0], chunk_of(i)[1], grouped_of[i])

        def vector_next_dcn(i):
            if is_child_step(i):
                dcn_of[i] = fs.tile([P, P, PACK], F32, name="dcn")
                fused(dcn_of[i][:], by_node(bank_of["nc", i]), 0.5, ALU.mult, m2dc_of[steps[i][0]][:], ALU.mult)

        def vector_quantise_child(i):
            if is_child_step(i):
                quantise_acts(steps[i][0], GATES + steps[i][1], df_of[i][:])

        def vector_gate_step(i):
            a = steps[i][0]
            to, tcc, ti, tu = tanh_out["o", i], tanh_out["c", i], tanh_out["i", i], tanh_out["u", i]
            diou = bfp.tile([P, GATES, P, PACK], BF16, name="diou", align_bytes=64)
            gho = xv.tile([P, P, PACK], F32, name="gho")
            back = xv.tile([P, P, PACK], F32, name="back")
            m2dc = xs.tile([P, P, PACK], F32, name="m2dc")
            oo = xv.tile([P, P, PACK], F32, name="oo")
            dsi = xv.tile([P, P, PACK], F32, name="dsi")
            ii = xv.tile([P, P, PACK], F32, name="ii")
            m2dc_of[a] = m2dc
            fused(gho[:], to[:], 1.0, ALU.add, by_node(bank_of["gh", i]), ALU.mult)
            vector_quantise_child(i - 1)
            fused(oo[:], to[:], -1.0, ALU.add, gho[:], ALU.mult)
            fused(back[:], square_out["c", i][:], -1.0, ALU.add, gho[:], ALU.mult)
            fused(diou[:, 1], oo[:], -0.25, ALU.mult, tcc[:], ALU.mult)
            if i == 0:
                vector_regroup(0)
            fused(m2dc[:], by_node(bank_of["gc", i]), -2.0, ALU.mult, back[:], ALU.add)
            vector_quantise_chunk(i)
            fused(dsi[:], ti[:], 1.0, ALU.add, m2dc[:], ALU.mult)
            vector_next_dcn(i + 1)
            fused(diou[:, 2], square_out["u", i][:], -0.25, ALU.add, dsi[:], ALU.mult)
            fused(ii[:], ti[:], -1.0, ALU.add, dsi[:], ALU.mult)
            vector_regroup(i + 1)
            fused(diou[:, 0], ii[:], 0.125, ALU.mult, tu[:], ALU.mult)
            quantise_acts(a, 1, diou[:, 1:3])
            quantise_acts(a, 0, diou[:, 0:1])

        def vector_child_step(i):
            vector_next_dcn(i + 1)
            vector_quantise_child(i - 1)
            df_of[i] = bfp.tile([P, 1, P, PACK], BF16, name="df", align_bytes=64)
            fused(df_of[i][:, 0], square_out["f", i][:], -0.25, ALU.add, dcn_of[i][:], ALU.mult)
            vector_regroup(i + 1)
            vector_quantise_chunk(i)

        with tc.manual_schedule():
            keep_clock_up(WARM_FIRST)
            for i in range(-LOAD_LEAD - 1, n_steps + 2):
                warm["count"] = 0 if i >= min(open_round[block] for block in blocks) else (1 if i + TANH_LEAD <= 0 else 2)
                loads(i + LOAD_LEAD)
                scalar_regroup(i + REGROUP_LEAD)
                for a, d in blocks:
                    if close_round[a, d] + 1 == i:
                        store(a, d, acc_of[a, d])
                square_part(i + SQUARE_LEAD)
                transposes16(i + T16_LEAD)
                tanh_part(i + TANH_LEAD)
                if i == -1:
                    vector_regroup(i)
                    vector_quantise_chunk(i)
                if is_gate_step(i):
                    vector_gate_step(i)
                if is_child_step(i):
                    vector_child_step(i)
                if i == n_steps:
                    vector_quantise_child(i - 1)
                for a, d in blocks:
                    if open_round[a, d] == i:
                        acc_of[a, d] = open_block(a, d)
                for a, d in blocks:
                    if close_round[a, d] == i:
                        close_block(a, d, acc_of[a, d])
